import numpy as np
import ml_dtypes


def mxq(x, axis, fmt="e4m3"):
    dtype, down = {"e4m3": (ml_dtypes.float8_e4m3fn, 7), "e5m2": (ml_dtypes.float8_e5m2, 14)}[fmt]
    v = np.moveaxis(np.asarray(x, np.float32).astype(ml_dtypes.bfloat16).astype(np.float64), axis, -1)
    blocks = v.reshape(v.shape[:-1] + (-1, 32))
    amax = np.abs(blocks).max(-1, keepdims=True)
    byte = np.maximum(np.where(amax > 0, np.frexp(amax)[1] - 1 + 127, 0) - down, 1)
    scale = np.exp2(byte - 127.0)
    codes = (blocks / scale).astype(np.float32).astype(dtype).astype(np.float64)
    return np.moveaxis((codes * scale).reshape(v.shape), -1, axis)


WIDE = False


def mx_kscale(k):
    if not WIDE:
        return np.ones(k)
    levels = np.array([10, -10, 5, -5, 0])
    a = np.random.permutation(np.resize(levels, k // 512 * 4)).reshape(k // 512, 4)
    idx = np.arange(k)
    return np.exp2(a[idx // 512, idx % 128 // 32])


BF16 = ml_dtypes.bfloat16


def bf(x):
    return np.asarray(x, np.float32).astype(BF16)


def f64(x):
    return np.asarray(x).astype(np.float64)


E2M1 = np.array([0.0, 0.5, 1.0, 1.5, 2.0, 3.0, 4.0, 6.0, -0.0, -0.5, -1.0, -1.5, -2.0, -3.0, -4.0, -6.0])


def pack_weight(w, fmt):
    k, n = w.shape
    w = f64(bf(w)).reshape(k // 32, 32, n)
    amax = np.abs(w).max(1)
    if fmt == "e4m3":
        byte = np.frexp(amax)[1] - 1 + 127 - 7
    else:
        mant, ex = np.frexp(amax / 6.0)
        byte = np.where(mant > 0.5, ex, ex - 1) + 127
    byte = np.clip(np.where(amax > 0, byte, 1), 1, 254)
    scaled = (w * np.exp2(127.0 - byte)[:, None, :]).reshape(k, n).astype(np.float32)
    by_word = np.ascontiguousarray(scaled.reshape(k // 512, 128, 4, n).transpose(0, 1, 3, 2))
    if fmt == "e4m3":
        words = by_word.astype(ml_dtypes.float8_e4m3fn).view(np.uint8)
    else:
        c = by_word.astype(ml_dtypes.float4_e2m1fn).view(np.uint8) & 0xF
        words = c[..., 0::2] | (c[..., 1::2] << 4)
    return np.ascontiguousarray(words), np.ascontiguousarray(byte.astype(np.uint8).reshape(k // 512, 16, n))


def unpack_weight(words, scales, fmt):
    g, p, n, _ = words.shape
    if fmt == "e4m3":
        vals = np.ascontiguousarray(words).view(ml_dtypes.float8_e4m3fn).astype(np.float64)
    else:
        nib = np.empty((g, p, n, 4), np.uint8)
        nib[..., 0::2] = words & 0xF
        nib[..., 1::2] = words >> 4
        vals = E2M1[nib]
    vals = vals * np.repeat(np.exp2(scales.astype(np.float64) - 127.0), 8, axis=1)[..., None]
    return vals.transpose(0, 1, 3, 2).reshape(g * 512, n)


B, D, T, N, H, DH = 4, 1024, 2048, 3, 2, 64
EPS = 1e-6
NEG_SLOPE = 0.2


def setup_inputs():
    s = mx_kscale(D)
    x = bf(np.random.standard_normal((B, D, T)) * s[:, None])
    stack = np.random.standard_normal((N, H, D, DH)) * 1.4 / np.sqrt(D) / s[:, None]
    words, scales = pack_weight(stack.reshape(-1, DH), "e4m3")
    norm_w = bf(1.5 + 0.1 * np.random.standard_normal(1))
    return {"x": x, "qkv_words": words, "qkv_scales": scales, "norm_w": norm_w}


def reference(x, qkv_words, qkv_scales, norm_w):
    x = f64(x)
    a = np.where(x >= 0, x, NEG_SLOPE * x)
    aq = mxq(a, 1, "e4m3")
    wq = unpack_weight(qkv_words, qkv_scales, "e4m3").reshape(N, H, D, DH)
    y = aq.transpose(0, 2, 1) @ wq.transpose(2, 0, 1, 3).reshape(D, N * H * DH)
    h = y.reshape(B, T, N, H, DH).transpose(2, 0, 3, 1, 4)
    denom = np.mean(h * h, axis=-2, keepdims=True)
    return f64(norm_w) * (h / np.sqrt(denom + EPS))

@@ -1,0 +1,230 @@
+from contextlib import ExitStack
+
+import concourse.mybir as mybir
+from concourse.masks import make_identity
+
+F32 = mybir.dt.float32
+BF16 = mybir.dt.bfloat16
+I32 = mybir.dt.int32
+U32 = mybir.dt.uint32
+U8 = mybir.dt.uint8
+FP8X4 = mybir.dt.float8_e4m3fn_x4
+ALU = mybir.AluOpType
+ACT = mybir.ActivationFunctionType
+
+BATCH, CHANNELS, SEQ = 4, 1024, 2048
+QKV, HEADS, HEAD_DIM = 3, 2, 64
+EPS = 1e-6
+NEG_SLOPE = 0.2
+
+P = 128
+PACK = 4
+K_PASS = P * PACK
+PASSES = CHANNELS // K_PASS
+MATRICES = QKV * HEADS
+W_COLS = MATRICES * HEAD_DIM
+UNIT_COLS = HEADS * HEAD_DIM
+CHUNK = 512
+CHUNKS = SEQ // CHUNK
+T_PER_PART = SEQ // P
+TR_PER_BANK = CHUNK // P
+PSUM_BANKS = 8
+
+FLOPS = 2 * BATCH * SEQ * CHANNELS * W_COLS
+
+
+def tile_mha_pa_t_e_kernel(tc, x, qkv_words, qkv_scales, norm_w, out):
+    nc = tc.nc
+    with ExitStack() as stack:
+        consts = stack.enter_context(tc.tile_pool(name="consts", bufs=1))
+        raw_pool = stack.enter_context(tc.tile_pool(name="raw", bufs=1))
+        grouped_pool = stack.enter_context(tc.tile_pool(name="grouped", bufs=3))
+        code_pool = stack.enter_context(tc.tile_pool(name="codes", bufs=2))
+        stat_pool = stack.enter_context(tc.tile_pool(name="stats", bufs=2))
+        normed_pool = stack.enter_context(tc.tile_pool(name="normed", bufs=2))
+        result_pool = stack.enter_context(tc.tile_pool(name="result", bufs=2))
+        psum = stack.enter_context(tc.psum_pool(name="psum", bufs=PSUM_BANKS))
+        stack.enter_context(tc.manual_schedule())
+
+        identity = consts.tile([P, P], F32)
+        make_identity(nc, identity[:])
+        eps = consts.tile([P, 1], F32)
+        nc.vector.memset(eps[:], EPS)
+        w_planes = consts.tile([P, PASSES, W_COLS], U8, align_bytes=64)
+        nc.vector.memset(w_planes[:].rearrange("p g c -> p (g c)").bitcast(I32), 0)
+        w_codes = consts.tile([P, PASSES, W_COLS], U32, align_bytes=64)
+        gain_bf16 = consts.tile([P, 1], BF16)
+        gain = consts.tile([P, 1], F32)
+        squares = consts.tile([P, CHUNK], BF16)
+        partial_copy = consts.tile([P, CHUNKS], F32)
+
+        raw = [
+            [raw_pool.tile([P, PACK, SEQ], BF16, name="raw%d%d" % (b, g)) for g in range(PASSES)]
+            for b in range(BATCH)
+        ]
+
+        def load_x(b, g, cols):
+            rows = x[b, g * K_PASS : (g + 1) * K_PASS, cols]
+            nc.sync.dma_start(out=raw[b][g][:, :, cols], in_=rows.rearrange("(p j) t -> p j t", j=PACK))
+
+        def load_weights():
+            words = qkv_words.rearrange("m p n t -> m p (n t)").bitcast(I32)
+            words = words.rearrange("(e g) p n -> g p e n", g=PASSES)
+            scales = qkv_scales.bitcast(I32).rearrange("(e g) q n -> g q e n", g=PASSES)
+            for g in range(PASSES):
+                nc.sync.dma_start(
+                    out=w_codes[:, g, :].bitcast(I32).rearrange("p (e n) -> p e n", e=MATRICES),
+                    in_=words[g],
+                )
+            for g in range(PASSES):
+                for quad in range(4):
+                    nc.sync.dma_start(
+                        out=w_planes[32 * quad : 32 * quad + 4, g, :]
+                        .bitcast(I32)
+                        .rearrange("r (e n) -> r e n", e=MATRICES),
+                        in_=scales[g, 4 * quad : 4 * quad + 4],
+                    )
+            nc.sync.dma_start(out=gain_bf16[:], in_=norm_w.partition_broadcast(P))
+
+        def chunk_cols(k):
+            return slice(k * CHUNK, (k + 1) * CHUNK)
+
+        for g in range(PASSES):
+            load_x(0, g, chunk_cols(0))
+        load_weights()
+        for k in range(1, CHUNKS):
+            for g in range(PASSES):
+                load_x(0, g, chunk_cols(k))
+        for b in range(1, BATCH):
+            for g in range(PASSES):
+                load_x(b, g, slice(0, SEQ))
+
+        nc.scalar.activation(out=partial_copy[:, 0:1], in_=eps[:], func=ACT.Abs_reciprocal_sqrt)
+        nc.scalar.copy(out=gain[:], in_=gain_bf16[:])
+
+        def leaky_relu(b, k, g):
+            grouped = grouped_pool.tile([P, CHUNK, PACK], BF16, align_bytes=64)
+            rows = raw[b][g][:, :, chunk_cols(k)].rearrange("p j t -> p t j")
+            nc.vector.scalar_tensor_tensor(
+                out=grouped[:], in0=rows, scalar=NEG_SLOPE, in1=rows, op0=ALU.mult, op1=ALU.max
+            )
+            return grouped
+
+        def quantise(grouped, codes, planes, g):
+            nc.vector.quantize_mx(
+                out=codes[:, g, :].bitcast(FP8X4),
+                scales=planes[:, g, :],
+                in_=grouped[:].rearrange("p t j -> p (t j)"),
+            )
+
+        def prepare(b):
+            quantised = []
+            late = None
+            for k in range(CHUNKS):
+                codes = code_pool.tile([P, PASSES, CHUNK], U32, tag="codes%d" % k, name="codes", align_bytes=64)
+                planes = code_pool.tile([P, PASSES, CHUNK], U8, tag="planes%d" % k, name="planes", align_bytes=64)
+                quantised.append((codes, planes))
+                for g in range(PASSES):
+                    grouped = leaky_relu(b, k, g)
+                    if late is not None:
+                        quantise(*late)
+                    late = (grouped, codes, planes, g)
+            quantise(*late)
+            return quantised
+
+        def multiply(n, codes, planes):
+            w_cols = slice(n * UNIT_COLS, (n + 1) * UNIT_COLS)
+            bank = psum.tile([P, CHUNK], F32, tag="bank", name="product")
+            for g in range(PASSES):
+                nc.tensor.matmul_mx(
+                    out=bank[:],
+                    lhsT=w_codes[:, g, w_cols].bitcast(FP8X4),
+                    lhsT_scale=w_planes[:, g, w_cols],
+                    rhs=codes[:, g, :].bitcast(FP8X4),
+                    rhs_scale=planes[:, g, :],
+                    start=(g == 0),
+                    stop=(g == PASSES - 1),
+                )
+            return bank
+
+        def add_squares(partial, quantised, k):
+            for n in range(QKV):
+                bank = multiply(n, *quantised[k])
+                nc.scalar.activation(
+                    out=squares[:], in_=bank[:], func=ACT.Square, accum_out=partial[:, n, k : k + 1]
+                )
+
+        def reciprocal_rms(partial):
+            total = stat_pool.tile([P, QKV], F32)
+            for n in range(QKV):
+                nc.scalar.activation(
+                    out=partial_copy[:], in_=partial[:, n, :], func=ACT.Copy, accum_out=total[:, n : n + 1]
+                )
+            rrms = stat_pool.tile([P, QKV], F32)
+            nc.scalar.activation(
+                out=rrms[:], in_=total[:], func=ACT.Abs_reciprocal_sqrt, scale=1.0 / SEQ, bias=eps[:]
+            )
+            return rrms
+
+        def empty_bank(index, shared, out_ap, in_ap, factor):
+            if shared and index % 2 == 1:
+                nc.vector.tensor_scalar(out=out_ap, in0=in_ap, scalar1=factor, scalar2=None, op0=ALU.mult)
+            else:
+                nc.scalar.activation(out=out_ap, in_=in_ap, func=ACT.Copy, scale=factor)
+
+        def normalise(n, quantised, rrms, shared):
+            normed = normed_pool.tile([P, T_PER_PART, P], F32)
+            rows_per_bank = CHUNK // T_PER_PART
+            for k in range(CHUNKS):
+                bank = multiply(n, *quantised[k])
+                empty_bank(
+                    k,
+                    shared,
+                    normed[:, :, k * rows_per_bank : (k + 1) * rows_per_bank],
+                    bank[:].rearrange("c (r s) -> c s r", s=T_PER_PART),
+                    rrms[:, n : n + 1],
+                )
+            return normed
+
+        def transpose_and_store(b, n, normed, shared):
+            result = result_pool.tile([P, HEADS, T_PER_PART, HEAD_DIM], F32)
+            for m in range(T_PER_PART // TR_PER_BANK):
+                bank = psum.tile([P, TR_PER_BANK, P], F32, tag="bank", name="flipped")
+                for s in range(TR_PER_BANK):
+                    nc.tensor.transpose(bank[:, s, :], normed[:, m * TR_PER_BANK + s, :], identity[:])
+                empty_bank(
+                    m,
+                    shared,
+                    result[:, :, m * TR_PER_BANK : (m + 1) * TR_PER_BANK, :].rearrange("r i s j -> r s i j"),
+                    bank[:].rearrange("r s (i j) -> r s i j", i=HEADS),
+                    gain[:],
+                )
+            nc.sync.dma_start(
+                out=out[n, b].rearrange("i (r s) j -> r i (s j)", s=T_PER_PART),
+                in_=result[:].rearrange("r i s j -> r i (s j)"),
+            )
+
+        quantised = prepare(0)
+        partial = stat_pool.tile([P, QKV, CHUNKS], F32)
+        for k in range(CHUNKS):
+            add_squares(partial, quantised, k)
+        rrms = reciprocal_rms(partial)
+        waiting = None
+        for b in range(BATCH):
+            last = b == BATCH - 1
+            if not last:
+                following = prepare(b + 1)
+                partial = stat_pool.tile([P, QKV, CHUNKS], F32)
+            for n in range(QKV):
+                normed = normalise(n, quantised, rrms, last)
+                if waiting is not None:
+                    transpose_and_store(*waiting, last)
+                waiting = (b, n, normed)
+                if not last:
+                    add_squares(partial, following, n)
+            if not last:
+                for k in range(QKV, CHUNKS):
+                    add_squares(partial, following, k)
+                rrms = reciprocal_rms(partial)
+                quantised = following
+        transpose_and_store(*waiting, True)

@@ -26,7 +26,6 @@ W_COLS = MATRICES * HEAD_DIM
 UNIT_COLS = HEADS * HEAD_DIM
 CHUNK = 512
 CHUNKS = SEQ // CHUNK
-T_PER_PART = SEQ // P
 TR_PER_BANK = CHUNK // P
 PSUM_BANKS = 8
 
@@ -173,36 +172,35 @@ def tile_mha_pa_t_e_kernel(tc, x, qkv_words, qkv_scales, norm_w, out):
                 nc.scalar.activation(out=out_ap, in_=in_ap, func=ACT.Copy, scale=factor)
 
         def normalise(n, quantised, rrms, shared):
-            normed = normed_pool.tile([P, T_PER_PART, P], F32)
-            rows_per_bank = CHUNK // T_PER_PART
+            normed = normed_pool.tile([P, CHUNKS, TR_PER_BANK, P], F32)
             for k in range(CHUNKS):
                 bank = multiply(n, *quantised[k])
                 empty_bank(
                     k,
                     shared,
-                    normed[:, :, k * rows_per_bank : (k + 1) * rows_per_bank],
-                    bank[:].rearrange("c (r s) -> c s r", s=T_PER_PART),
+                    normed[:, k, :, :].rearrange("c s r -> c r s"),
+                    bank[:].rearrange("c (r s) -> c r s", s=TR_PER_BANK),
                     rrms[:, n : n + 1],
                 )
             return normed
 
         def transpose_and_store(b, n, normed, shared):
-            result = result_pool.tile([P, HEADS, T_PER_PART, HEAD_DIM], F32)
-            for m in range(T_PER_PART // TR_PER_BANK):
+            result = result_pool.tile([P, HEADS, CHUNKS, TR_PER_BANK, HEAD_DIM], F32)
+            for k in range(CHUNKS):
                 bank = psum.tile([P, TR_PER_BANK, P], F32, tag="bank", name="flipped")
                 for s in range(TR_PER_BANK):
-                    nc.tensor.transpose(bank[:, s, :], normed[:, m * TR_PER_BANK + s, :], identity[:])
+                    nc.tensor.transpose(bank[:, s, :], normed[:, k, s, :], identity[:])
                 empty_bank(
-                    m,
+                    k,
                     shared,
-                    result[:, :, m * TR_PER_BANK : (m + 1) * TR_PER_BANK, :].rearrange("r i s j -> r s i j"),
+                    result[:, :, k, :, :].rearrange("r i s j -> r s i j"),
                     bank[:].rearrange("r s (i j) -> r s i j", i=HEADS),
                     gain[:],
                 )
-            nc.sync.dma_start(
-                out=out[n, b].rearrange("i (r s) j -> r i (s j)", s=T_PER_PART),
-                in_=result[:].rearrange("r i s j -> r i (s j)"),
-            )
+                nc.sync.dma_start(
+                    out=out[n, b, :, chunk_cols(k), :].rearrange("i (r s) j -> r i (s j)", s=TR_PER_BANK),
+                    in_=result[:, :, k, :, :].rearrange("r i s j -> r i (s j)"),
+                )
 
         quantised = prepare(0)
         partial = stat_pool.tile([P, QKV, CHUNKS], F32)

@@ -38,6 +38,8 @@ def tile_mha_pa_t_e_kernel(tc, x, qkv_words, qkv_scales, norm_w, out):
         consts = stack.enter_context(tc.tile_pool(name="consts", bufs=1))
         raw_pool = stack.enter_context(tc.tile_pool(name="raw", bufs=1))
         grouped_pool = stack.enter_context(tc.tile_pool(name="grouped", bufs=3))
+        lifted_pool = stack.enter_context(tc.tile_pool(name="lifted", bufs=2))
+        scaled_pool = stack.enter_context(tc.tile_pool(name="scaled", bufs=1))
         code_pool = stack.enter_context(tc.tile_pool(name="codes", bufs=2))
         stat_pool = stack.enter_context(tc.tile_pool(name="stats", bufs=2))
         normed_pool = stack.enter_context(tc.tile_pool(name="normed", bufs=2))
@@ -109,27 +111,71 @@ def tile_mha_pa_t_e_kernel(tc, x, qkv_words, qkv_scales, norm_w, out):
             )
             return grouped
 
-        def quantise(grouped, codes, planes, g):
+        def regroup_on_scalar(b, k, g):
+            lifted = lifted_pool.tile([P, CHUNK, PACK], BF16, align_bytes=64)
+            nc.scalar.copy(out=lifted[:], in_=raw[b][g][:, :, chunk_cols(k)].rearrange("p j t -> p t j"))
+            return lifted
+
+        def scale_down(lifted, holder):
+            scaled = scaled_pool.tile([P, CHUNK * PACK], BF16)
+            holder.append(scaled)
+            nc.vector.tensor_scalar(
+                out=scaled[:],
+                in0=lifted[:].rearrange("p t j -> p (t j)"),
+                scalar1=NEG_SLOPE,
+                scalar2=None,
+                op0=ALU.mult,
+            )
+
+        def take_larger(lifted, holder):
+            flat = lifted[:].rearrange("p t j -> p (t j)")
+            nc.vector.tensor_tensor(out=flat, in0=flat, in1=holder[0][:], op=ALU.max)
+
+        quantised = {}
+        passes_ready = {}
+
+        def quantise(grouped, b, k, g):
+            if g == 0:
+                codes = code_pool.tile([P, PASSES, CHUNK], U32, tag="codes%d" % k, name="codes", align_bytes=64)
+                planes = code_pool.tile([P, PASSES, CHUNK], U8, tag="planes%d" % k, name="planes", align_bytes=64)
+                quantised[(b, k)] = (codes, planes)
+            codes, planes = quantised[(b, k)]
             nc.vector.quantize_mx(
                 out=codes[:, g, :].bitcast(FP8X4),
                 scales=planes[:, g, :],
                 in_=grouped[:].rearrange("p t j -> p (t j)"),
             )
+            passes_ready[(b, k)] = g + 1
 
-        def prepare(b):
-            quantised = []
-            late = None
-            for k in range(CHUNKS):
-                codes = code_pool.tile([P, PASSES, CHUNK], U32, tag="codes%d" % k, name="codes", align_bytes=64)
-                planes = code_pool.tile([P, PASSES, CHUNK], U8, tag="planes%d" % k, name="planes", align_bytes=64)
-                quantised.append((codes, planes))
-                for g in range(PASSES):
-                    grouped = leaky_relu(b, k, g)
-                    if late is not None:
-                        quantise(*late)
-                    late = (grouped, codes, planes, g)
-            quantise(*late)
-            return quantised
+        pieces = [(b, k, g) for b in range(BATCH) for k in range(CHUNKS) for g in range(PASSES)]
+        started = [0]
+        unfinished = []
+
+        def advance():
+            for steps in unfinished:
+                step, arguments = steps.pop(0)
+                step(*arguments)
+            for steps in [s for s in unfinished if not s]:
+                unfinished.remove(steps)
+
+        def start_next_piece():
+            b, k, g = pieces[started[0]]
+            started[0] += 1
+            if b == 0 and g == 1:
+                lifted = regroup_on_scalar(b, k, g)
+                holder = []
+                steps = [(scale_down, (lifted, holder)), (take_larger, (lifted, holder)), (quantise, (lifted, b, k, g))]
+            else:
+                steps = [(quantise, (leaky_relu(b, k, g), b, k, g))]
+            advance()
+            unfinished.append(steps)
+
+        def ensure(b, k):
+            while passes_ready.get((b, k), 0) < PASSES:
+                if started[0] < len(pieces):
+                    start_next_piece()
+                else:
+                    advance()
 
         def multiply(n, codes, planes):
             w_cols = slice(n * UNIT_COLS, (n + 1) * UNIT_COLS)
@@ -146,9 +192,10 @@ def tile_mha_pa_t_e_kernel(tc, x, qkv_words, qkv_scales, norm_w, out):
                 )
             return bank
 
-        def add_squares(partial, quantised, k):
+        def add_squares(partial, b, k):
+            ensure(b, k)
             for n in range(QKV):
-                bank = multiply(n, *quantised[k])
+                bank = multiply(n, *quantised[(b, k)])
                 nc.scalar.activation(
                     out=squares[:], in_=bank[:], func=ACT.Square, accum_out=partial[:, n, k : k + 1]
                 )
@@ -171,10 +218,10 @@ def tile_mha_pa_t_e_kernel(tc, x, qkv_words, qkv_scales, norm_w, out):
             else:
                 nc.scalar.activation(out=out_ap, in_=in_ap, func=ACT.Copy, scale=factor)
 
-        def normalise(n, quantised, rrms, shared):
+        def normalise(b, n, rrms, shared):
             normed = normed_pool.tile([P, CHUNKS, TR_PER_BANK, P], F32)
             for k in range(CHUNKS):
-                bank = multiply(n, *quantised[k])
+                bank = multiply(n, *quantised[(b, k)])
                 empty_bank(
                     k,
                     shared,
@@ -202,27 +249,24 @@ def tile_mha_pa_t_e_kernel(tc, x, qkv_words, qkv_scales, norm_w, out):
                     in_=result[:, :, k, :, :].rearrange("r i s j -> r i (s j)"),
                 )
 
-        quantised = prepare(0)
         partial = stat_pool.tile([P, QKV, CHUNKS], F32)
         for k in range(CHUNKS):
-            add_squares(partial, quantised, k)
+            add_squares(partial, 0, k)
         rrms = reciprocal_rms(partial)
         waiting = None
         for b in range(BATCH):
             last = b == BATCH - 1
             if not last:
-                following = prepare(b + 1)
                 partial = stat_pool.tile([P, QKV, CHUNKS], F32)
             for n in range(QKV):
-                normed = normalise(n, quantised, rrms, last)
+                normed = normalise(b, n, rrms, last)
                 if waiting is not None:
                     transpose_and_store(*waiting, last)
                 waiting = (b, n, normed)
                 if not last:
-                    add_squares(partial, following, n)
+                    add_squares(partial, b + 1, n)
             if not last:
                 for k in range(QKV, CHUNKS):
-                    add_squares(partial, following, k)
+                    add_squares(partial, b + 1, k)
                 rrms = reciprocal_rms(partial)
-                quantised = following
         transpose_and_store(*waiting, True)

@@ -37,14 +37,14 @@ def tile_mha_pa_t_e_kernel(tc, x, qkv_words, qkv_scales, norm_w, out):
     with ExitStack() as stack:
         consts = stack.enter_context(tc.tile_pool(name="consts", bufs=1))
         raw_pool = stack.enter_context(tc.tile_pool(name="raw", bufs=1))
-        grouped_pool = stack.enter_context(tc.tile_pool(name="grouped", bufs=3))
-        lifted_pool = stack.enter_context(tc.tile_pool(name="lifted", bufs=2))
+        grouped_pool = stack.enter_context(tc.tile_pool(name="grouped", bufs=2))
+        lifted_pool = stack.enter_context(tc.tile_pool(name="lifted", bufs=3))
         scaled_pool = stack.enter_context(tc.tile_pool(name="scaled", bufs=1))
         code_pool = stack.enter_context(tc.tile_pool(name="codes", bufs=2))
         stat_pool = stack.enter_context(tc.tile_pool(name="stats", bufs=2))
-        normed_pool = stack.enter_context(tc.tile_pool(name="normed", bufs=2))
-        result_pool = stack.enter_context(tc.tile_pool(name="result", bufs=2))
-        psum = stack.enter_context(tc.psum_pool(name="psum", bufs=PSUM_BANKS))
+        normed_pool = stack.enter_context(tc.tile_pool(name="normed", bufs=8))
+        result_pool = stack.enter_context(tc.tile_pool(name="result", bufs=8))
+        psum = stack.enter_context(tc.psum_pool(name="psum", bufs=1))
         stack.enter_context(tc.manual_schedule())
 
         identity = consts.tile([P, P], F32)
@@ -90,18 +90,16 @@ def tile_mha_pa_t_e_kernel(tc, x, qkv_words, qkv_scales, norm_w, out):
         def chunk_cols(k):
             return slice(k * CHUNK, (k + 1) * CHUNK)
 
-        for g in range(PASSES):
-            load_x(0, g, chunk_cols(0))
-        load_weights()
-        for k in range(1, CHUNKS):
+        for k in range(CHUNKS):
             for g in range(PASSES):
                 load_x(0, g, chunk_cols(k))
+        load_weights()
         for b in range(1, BATCH):
             for g in range(PASSES):
                 load_x(b, g, slice(0, SEQ))
 
         nc.scalar.activation(out=partial_copy[:, 0:1], in_=eps[:], func=ACT.Abs_reciprocal_sqrt)
-        nc.scalar.copy(out=gain[:], in_=gain_bf16[:])
+        nc.gpsimd.tensor_copy(out=gain[:], in_=gain_bf16[:])
 
         def leaky_relu(b, k, g):
             grouped = grouped_pool.tile([P, CHUNK, PACK], BF16, align_bytes=64)
@@ -135,7 +133,7 @@ def tile_mha_pa_t_e_kernel(tc, x, qkv_words, qkv_scales, norm_w, out):
         passes_ready = {}
 
         def quantise(grouped, b, k, g):
-            if g == 0:
+            if (b, k) not in quantised:
                 codes = code_pool.tile([P, PASSES, CHUNK], U32, tag="codes%d" % k, name="codes", align_bytes=64)
                 planes = code_pool.tile([P, PASSES, CHUNK], U8, tag="planes%d" % k, name="planes", align_bytes=64)
                 quantised[(b, k)] = (codes, planes)
@@ -145,7 +143,7 @@ def tile_mha_pa_t_e_kernel(tc, x, qkv_words, qkv_scales, norm_w, out):
                 scales=planes[:, g, :],
                 in_=grouped[:].rearrange("p t j -> p (t j)"),
             )
-            passes_ready[(b, k)] = g + 1
+            passes_ready[(b, k)] = passes_ready.get((b, k), 0) + 1
 
         pieces = [(b, k, g) for b in range(BATCH) for k in range(CHUNKS) for g in range(PASSES)]
         started = [0]
@@ -161,112 +159,169 @@ def tile_mha_pa_t_e_kernel(tc, x, qkv_words, qkv_scales, norm_w, out):
         def start_next_piece():
             b, k, g = pieces[started[0]]
             started[0] += 1
-            if b == 0 and g == 1:
+            if b == 0 and g == (0 if k == CHUNKS - 1 else 1):
+                advance()
                 lifted = regroup_on_scalar(b, k, g)
                 holder = []
                 steps = [(scale_down, (lifted, holder)), (take_larger, (lifted, holder)), (quantise, (lifted, b, k, g))]
             else:
                 steps = [(quantise, (leaky_relu(b, k, g), b, k, g))]
-            advance()
+                advance()
             unfinished.append(steps)
 
         def ensure(b, k):
             while passes_ready.get((b, k), 0) < PASSES:
-                if started[0] < len(pieces):
+                if started[0] < len(pieces) and pieces[started[0]][0] == b:
                     start_next_piece()
                 else:
                     advance()
 
-        def multiply(n, codes, planes):
-            w_cols = slice(n * UNIT_COLS, (n + 1) * UNIT_COLS)
-            bank = psum.tile([P, CHUNK], F32, tag="bank", name="product")
+        ring = [0]
+        held = []
+
+        def take_bank(shape, name, index=None):
+            if index is None:
+                while ring[0] % PSUM_BANKS in held:
+                    ring[0] += 1
+                index = ring[0] % PSUM_BANKS
+                ring[0] += 1
+            return index, psum.tile(shape, F32, tag="bank%d" % index, name=name)
+
+        def multiply(units, b, k, index=None):
+            codes, planes = quantised[(b, k)]
+            banks = [take_bank([P, CHUNK], "product", index) for n in units]
             for g in range(PASSES):
-                nc.tensor.matmul_mx(
-                    out=bank[:],
-                    lhsT=w_codes[:, g, w_cols].bitcast(FP8X4),
-                    lhsT_scale=w_planes[:, g, w_cols],
-                    rhs=codes[:, g, :].bitcast(FP8X4),
-                    rhs_scale=planes[:, g, :],
-                    start=(g == 0),
-                    stop=(g == PASSES - 1),
-                )
-            return bank
+                for n, (place, bank) in zip(units, banks):
+                    w_cols = slice(n * UNIT_COLS, (n + 1) * UNIT_COLS)
+                    nc.tensor.matmul_mx(
+                        out=bank[:],
+                        lhsT=w_codes[:, g, w_cols].bitcast(FP8X4),
+                        lhsT_scale=w_planes[:, g, w_cols],
+                        rhs=codes[:, g, :].bitcast(FP8X4),
+                        rhs_scale=planes[:, g, :],
+                        start=(g == 0),
+                        stop=(g == PASSES - 1),
+                    )
+            return banks
 
         def add_squares(partial, b, k):
             ensure(b, k)
-            for n in range(QKV):
-                bank = multiply(n, *quantised[(b, k)])
+            banks = multiply(range(QKV), b, k)
+            for n, (place, bank) in enumerate(banks):
                 nc.scalar.activation(
                     out=squares[:], in_=bank[:], func=ACT.Square, accum_out=partial[:, n, k : k + 1]
                 )
+            return banks
 
-        def reciprocal_rms(partial):
+        def reciprocal_rms(partial, on_vector):
             total = stat_pool.tile([P, QKV], F32)
-            for n in range(QKV):
-                nc.scalar.activation(
-                    out=partial_copy[:], in_=partial[:, n, :], func=ACT.Copy, accum_out=total[:, n : n + 1]
-                )
+            if on_vector:
+                nc.vector.tensor_reduce(out=total[:], in_=partial[:], axis=mybir.AxisListType.X, op=ALU.add)
+            else:
+                for n in range(QKV):
+                    nc.scalar.activation(
+                        out=partial_copy[:], in_=partial[:, n, :], func=ACT.Copy, accum_out=total[:, n : n + 1]
+                    )
             rrms = stat_pool.tile([P, QKV], F32)
             nc.scalar.activation(
                 out=rrms[:], in_=total[:], func=ACT.Abs_reciprocal_sqrt, scale=1.0 / SEQ, bias=eps[:]
             )
             return rrms
 
-        def empty_bank(index, shared, out_ap, in_ap, factor):
-            if shared and index % 2 == 1:
+        def empty_bank(on_vector, out_ap, in_ap, factor):
+            if on_vector:
                 nc.vector.tensor_scalar(out=out_ap, in0=in_ap, scalar1=factor, scalar2=None, op0=ALU.mult)
             else:
                 nc.scalar.activation(out=out_ap, in_=in_ap, func=ACT.Copy, scale=factor)
 
-        def normalise(b, n, rrms, shared):
-            normed = normed_pool.tile([P, CHUNKS, TR_PER_BANK, P], F32)
-            for k in range(CHUNKS):
-                bank = multiply(n, *quantised[(b, k)])
-                empty_bank(
-                    k,
-                    shared,
-                    normed[:, k, :, :].rearrange("c s r -> c r s"),
-                    bank[:].rearrange("c (r s) -> c r s", s=TR_PER_BANK),
-                    rrms[:, n : n + 1],
-                )
+        def normalise(n, bank, rrms, on_vector):
+            normed = normed_pool.tile([P, TR_PER_BANK, P], F32)
+            empty_bank(
+                on_vector,
+                normed[:].rearrange("c s r -> c r s"),
+                bank[:].rearrange("c (r s) -> c r s", s=TR_PER_BANK),
+                rrms[:, n : n + 1],
+            )
             return normed
 
-        def transpose_and_store(b, n, normed, shared):
-            result = result_pool.tile([P, HEADS, CHUNKS, TR_PER_BANK, HEAD_DIM], F32)
-            for k in range(CHUNKS):
-                bank = psum.tile([P, TR_PER_BANK, P], F32, tag="bank", name="flipped")
-                for s in range(TR_PER_BANK):
-                    nc.tensor.transpose(bank[:, s, :], normed[:, k, s, :], identity[:])
-                empty_bank(
-                    k,
-                    shared,
-                    result[:, :, k, :, :].rearrange("r i s j -> r s i j"),
-                    bank[:].rearrange("r s (i j) -> r s i j", i=HEADS),
-                    gain[:],
-                )
-                nc.sync.dma_start(
-                    out=out[n, b, :, chunk_cols(k), :].rearrange("i (r s) j -> r i (s j)", s=TR_PER_BANK),
-                    in_=result[:, :, k, :, :].rearrange("r i s j -> r i (s j)"),
-                )
+        def flip(normed, index=None):
+            place, bank = take_bank([P, TR_PER_BANK, P], "flipped", index)
+            for s in range(TR_PER_BANK):
+                nc.tensor.transpose(bank[:, s, :], normed[:, s, :], identity[:])
+            return bank
 
+        def store(b, n, k, bank, on_vector):
+            result = result_pool.tile([P, HEADS, TR_PER_BANK, HEAD_DIM], F32)
+            empty_bank(
+                on_vector,
+                result[:].rearrange("r i s j -> r s i j"),
+                bank[:].rearrange("r s (i j) -> r s i j", i=HEADS),
+                gain[:],
+            )
+            nc.sync.dma_start(
+                out=out[n, b, :, chunk_cols(k), :].rearrange("i (r s) j -> r i (s j)", s=TR_PER_BANK),
+                in_=result[:].rearrange("r i s j -> r i (s j)"),
+            )
+
+        def normalise_unit(b, n, rrms):
+            return [normalise(n, multiply([n], b, k)[0][1], rrms, False) for k in range(CHUNKS)]
+
+        def flip_and_store_unit(b, n, normed):
+            for k in range(CHUNKS):
+                store(b, n, k, flip(normed[k]), False)
+
+        LAST = BATCH - 1
         partial = stat_pool.tile([P, QKV, CHUNKS], F32)
+        ensure(0, CHUNKS - 1)
         for k in range(CHUNKS):
             add_squares(partial, 0, k)
-        rrms = reciprocal_rms(partial)
+        rrms = reciprocal_rms(partial, False)
         waiting = None
-        for b in range(BATCH):
-            last = b == BATCH - 1
-            if not last:
-                partial = stat_pool.tile([P, QKV, CHUNKS], F32)
-            for n in range(QKV):
-                normed = normalise(b, n, rrms, last)
-                if waiting is not None:
-                    transpose_and_store(*waiting, last)
-                waiting = (b, n, normed)
-                if not last:
-                    add_squares(partial, b + 1, n)
-            if not last:
-                for k in range(QKV, CHUNKS):
-                    add_squares(partial, b + 1, k)
-                rrms = reciprocal_rms(partial)
-        transpose_and_store(*waiting, True)
+        kept = []
+        for b in range(LAST):
+            partial = stat_pool.tile([P, QKV, CHUNKS], F32)
+            for k in range(CHUNKS):
+                if k < QKV:
+                    normed = normalise_unit(b, k, rrms)
+                    if waiting is not None:
+                        flip_and_store_unit(*waiting)
+                    waiting = (b, k, normed)
+                keep = b + 1 == LAST and k >= CHUNKS - 2
+                if keep and waiting is not None:
+                    flip_and_store_unit(*waiting)
+                    waiting = None
+                if keep and k == CHUNKS - 1:
+                    for n in range(PSUM_BANKS - 2 * QKV):
+                        place, bank = multiply([n], LAST, 0)[0]
+                        held.append(place)
+                        kept.append((0, n, place, bank))
+                banks = add_squares(partial, b + 1, k)
+                if keep:
+                    for n, (place, bank) in enumerate(banks):
+                        held.append(place)
+                        kept.append((k, n, place, bank))
+            rrms = reciprocal_rms(partial, b + 1 == LAST)
+
+        items = list(kept)
+        missing = [(k, n) for k in range(CHUNKS) for n in range(QKV) if (k, n) not in [item[:2] for item in kept]]
+        flipped = {}
+
+        def normalise_and_flip(i):
+            k, n, place, bank = items[i]
+            flipped[i] = flip(normalise(n, bank, rrms, i % 2 == 1), place)
+
+        def store_item(i):
+            k, n, place, bank = items[i]
+            store(LAST, n, k, flipped[i], i % 2 == 1)
+
+        for i in range(len(kept)):
+            normalise_and_flip(i)
+        for i, (k, n) in enumerate(missing):
+            store_item(i)
+            place, bank = multiply([n], LAST, k, items[i][2])[0]
+            items.append((k, n, place, bank))
+        for i in range(len(missing)):
+            normalise_and_flip(len(kept) + i)
+            store_item(len(missing) + i)
+        for i in range(len(kept), len(items)):
+            store_item(i)

@@ -238,8 +238,8 @@ def tile_mha_pa_t_e_kernel(tc, x, qkv_words, qkv_scales, norm_w, out):
             normed = normed_pool.tile([P, TR_PER_BANK, P], F32)
             empty_bank(
                 on_vector,
-                normed[:].rearrange("c s r -> c r s"),
-                bank[:].rearrange("c (r s) -> c r s", s=TR_PER_BANK),
+                normed[:],
+                bank[:].rearrange("c (r s) -> c s r", s=TR_PER_BANK),
                 rrms[:, n : n + 1],
             )
             return normed

@@ -45,7 +45,6 @@ def tile_mha_pa_t_e_kernel(tc, x, qkv_words, qkv_scales, norm_w, out):
         normed_pool = stack.enter_context(tc.tile_pool(name="normed", bufs=8))
         result_pool = stack.enter_context(tc.tile_pool(name="result", bufs=8))
         psum = stack.enter_context(tc.psum_pool(name="psum", bufs=1))
-        stack.enter_context(tc.manual_schedule())
 
         identity = consts.tile([P, P], F32)
         make_identity(nc, identity[:])

@@ -28,6 +28,7 @@ CHUNK = 512
 CHUNKS = SEQ // CHUNK
 TR_PER_BANK = CHUNK // P
 PSUM_BANKS = 8
+RAW_ROWS = 3
 
 FLOPS = 2 * BATCH * SEQ * CHANNELS * W_COLS
 
@@ -37,10 +38,10 @@ def tile_mha_pa_t_e_kernel(tc, x, qkv_words, qkv_scales, norm_w, out):
     with ExitStack() as stack:
         consts = stack.enter_context(tc.tile_pool(name="consts", bufs=1))
         raw_pool = stack.enter_context(tc.tile_pool(name="raw", bufs=1))
-        grouped_pool = stack.enter_context(tc.tile_pool(name="grouped", bufs=2))
+        grouped_pool = stack.enter_context(tc.tile_pool(name="grouped", bufs=4))
         lifted_pool = stack.enter_context(tc.tile_pool(name="lifted", bufs=3))
         scaled_pool = stack.enter_context(tc.tile_pool(name="scaled", bufs=1))
-        code_pool = stack.enter_context(tc.tile_pool(name="codes", bufs=2))
+        code_pool = stack.enter_context(tc.tile_pool(name="codes", bufs=3))
         stat_pool = stack.enter_context(tc.tile_pool(name="stats", bufs=2))
         normed_pool = stack.enter_context(tc.tile_pool(name="normed", bufs=8))
         result_pool = stack.enter_context(tc.tile_pool(name="result", bufs=8))
@@ -58,14 +59,15 @@ def tile_mha_pa_t_e_kernel(tc, x, qkv_words, qkv_scales, norm_w, out):
         squares = consts.tile([P, CHUNK], BF16)
         partial_copy = consts.tile([P, CHUNKS], F32)
 
-        raw = [
-            [raw_pool.tile([P, PACK, SEQ], BF16, name="raw%d%d" % (b, g)) for g in range(PASSES)]
-            for b in range(BATCH)
-        ]
+        raw = {}
+
+        def make_room(b):
+            for g in range(PASSES):
+                raw[(b, g)] = raw_pool.tile([P, PACK, SEQ], BF16, name="raw%d%d" % (b % RAW_ROWS, g))
 
         def load_x(b, g, cols):
             rows = x[b, g * K_PASS : (g + 1) * K_PASS, cols]
-            nc.sync.dma_start(out=raw[b][g][:, :, cols], in_=rows.rearrange("(p j) t -> p j t", j=PACK))
+            nc.sync.dma_start(out=raw[(b, g)][:, :, cols], in_=rows.rearrange("(p j) t -> p j t", j=PACK))
 
         def load_weights():
             words = qkv_words.rearrange("m p n t -> m p (n t)").bitcast(I32)
@@ -89,11 +91,13 @@ def tile_mha_pa_t_e_kernel(tc, x, qkv_words, qkv_scales, norm_w, out):
         def chunk_cols(k):
             return slice(k * CHUNK, (k + 1) * CHUNK)
 
+        make_room(0)
         for k in range(CHUNKS):
             for g in range(PASSES):
                 load_x(0, g, chunk_cols(k))
         load_weights()
-        for b in range(1, BATCH):
+        for b in range(1, RAW_ROWS):
+            make_room(b)
             for g in range(PASSES):
                 load_x(b, g, slice(0, SEQ))
 
@@ -102,7 +106,7 @@ def tile_mha_pa_t_e_kernel(tc, x, qkv_words, qkv_scales, norm_w, out):
 
         def leaky_relu(b, k, g):
             grouped = grouped_pool.tile([P, CHUNK, PACK], BF16, align_bytes=64)
-            rows = raw[b][g][:, :, chunk_cols(k)].rearrange("p j t -> p t j")
+            rows = raw[(b, g)][:, :, chunk_cols(k)].rearrange("p j t -> p t j")
             nc.vector.scalar_tensor_tensor(
                 out=grouped[:], in0=rows, scalar=NEG_SLOPE, in1=rows, op0=ALU.mult, op1=ALU.max
             )
@@ -110,7 +114,7 @@ def tile_mha_pa_t_e_kernel(tc, x, qkv_words, qkv_scales, norm_w, out):
 
         def regroup_on_scalar(b, k, g):
             lifted = lifted_pool.tile([P, CHUNK, PACK], BF16, align_bytes=64)
-            nc.scalar.copy(out=lifted[:], in_=raw[b][g][:, :, chunk_cols(k)].rearrange("p j t -> p t j"))
+            nc.scalar.copy(out=lifted[:], in_=raw[(b, g)][:, :, chunk_cols(k)].rearrange("p j t -> p t j"))
             return lifted
 
         def scale_down(lifted, holder):
@@ -272,6 +276,10 @@ def tile_mha_pa_t_e_kernel(tc, x, qkv_words, qkv_scales, norm_w, out):
         LAST = BATCH - 1
         partial = stat_pool.tile([P, QKV, CHUNKS], F32)
         ensure(0, CHUNKS - 1)
+        for b in range(RAW_ROWS, BATCH):
+            make_room(b)
+            for g in range(PASSES):
+                load_x(b, g, slice(0, SEQ))
         for k in range(CHUNKS):
             add_squares(partial, 0, k)
         rrms = reciprocal_rms(partial, False)

@@ -45,7 +45,7 @@ def tile_mha_pa_t_e_kernel(tc, x, qkv_words, qkv_scales, norm_w, out):
         stat_pool = stack.enter_context(tc.tile_pool(name="stats", bufs=2))
         normed_pool = stack.enter_context(tc.tile_pool(name="normed", bufs=8))
         result_pool = stack.enter_context(tc.tile_pool(name="result", bufs=8))
-        psum = stack.enter_context(tc.psum_pool(name="psum", bufs=1))
+        psum = stack.enter_context(tc.psum_pool(name="psum", bufs=PSUM_BANKS))
 
         identity = consts.tile([P, P], F32)
         make_identity(nc, identity[:])
@@ -179,16 +179,8 @@ def tile_mha_pa_t_e_kernel(tc, x, qkv_words, qkv_scales, norm_w, out):
                 else:
                     advance()
 
-        ring = [0]
-        held = []
-
         def take_bank(shape, name, index=None):
-            if index is None:
-                while ring[0] % PSUM_BANKS in held:
-                    ring[0] += 1
-                index = ring[0] % PSUM_BANKS
-                ring[0] += 1
-            return index, psum.tile(shape, F32, tag="bank%d" % index, name=name)
+            return index, psum.tile(shape, F32, tag="bank", name=name)
 
         def multiply(units, b, k, index=None):
             codes, planes = quantised[(b, k)]
@@ -300,12 +292,10 @@ def tile_mha_pa_t_e_kernel(tc, x, qkv_words, qkv_scales, norm_w, out):
                 if keep and k == CHUNKS - 1:
                     for n in range(PSUM_BANKS - 2 * QKV):
                         place, bank = multiply([n], LAST, 0)[0]
-                        held.append(place)
                         kept.append((0, n, place, bank))
                 banks = add_squares(partial, b + 1, k)
                 if keep:
                     for n, (place, bank) in enumerate(banks):
-                        held.append(place)
                         kept.append((k, n, place, bank))
             rrms = reciprocal_rms(partial, b + 1 == LAST)
 

from contextlib import ExitStack

import concourse.mybir as mybir
from concourse.masks import make_identity

F32 = mybir.dt.float32
BF16 = mybir.dt.bfloat16
I32 = mybir.dt.int32
U32 = mybir.dt.uint32
U8 = mybir.dt.uint8
FP8X4 = mybir.dt.float8_e4m3fn_x4
ALU = mybir.AluOpType
ACT = mybir.ActivationFunctionType

BATCH, CHANNELS, SEQ = 4, 1024, 2048
QKV, HEADS, HEAD_DIM = 3, 2, 64
EPS = 1e-6
NEG_SLOPE = 0.2

P = 128
PACK = 4
K_PASS = P * PACK
PASSES = CHANNELS // K_PASS
MATRICES = QKV * HEADS
W_COLS = MATRICES * HEAD_DIM
UNIT_COLS = HEADS * HEAD_DIM
CHUNK = 512
CHUNKS = SEQ // CHUNK
TR_PER_BANK = CHUNK // P
PSUM_BANKS = 8
RAW_ROWS = 3

FLOPS = 2 * BATCH * SEQ * CHANNELS * W_COLS


def tile_mha_pa_t_e_kernel(tc, x, qkv_words, qkv_scales, norm_w, out):
    nc = tc.nc
    with ExitStack() as stack:
        consts = stack.enter_context(tc.tile_pool(name="consts", bufs=1))
        raw_pool = stack.enter_context(tc.tile_pool(name="raw", bufs=1))
        grouped_pool = stack.enter_context(tc.tile_pool(name="grouped", bufs=4))
        lifted_pool = stack.enter_context(tc.tile_pool(name="lifted", bufs=3))
        scaled_pool = stack.enter_context(tc.tile_pool(name="scaled", bufs=1))
        code_pool = stack.enter_context(tc.tile_pool(name="codes", bufs=3))
        stat_pool = stack.enter_context(tc.tile_pool(name="stats", bufs=2))
        normed_pool = stack.enter_context(tc.tile_pool(name="normed", bufs=8))
        result_pool = stack.enter_context(tc.tile_pool(name="result", bufs=8))
        psum = stack.enter_context(tc.psum_pool(name="psum", bufs=PSUM_BANKS))

        identity = consts.tile([P, P], F32)
        make_identity(nc, identity[:])
        eps = consts.tile([P, 1], F32)
        nc.vector.memset(eps[:], EPS)
        w_planes = consts.tile([P, PASSES, W_COLS], U8, align_bytes=64)
        nc.vector.memset(w_planes[:].rearrange("p g c -> p (g c)").bitcast(I32), 0)
        w_codes = consts.tile([P, PASSES, W_COLS], U32, align_bytes=64)
        gain_bf16 = consts.tile([P, 1], BF16)
        gain = consts.tile([P, 1], F32)
        squares = consts.tile([P, CHUNK], BF16)
        partial_copy = consts.tile([P, CHUNKS], F32)

        raw = {}

        def make_room(b):
            for g in range(PASSES):
                raw[(b, g)] = raw_pool.tile([P, PACK, SEQ], BF16, name="raw%d%d" % (b % RAW_ROWS, g))

        def load_x(b, g, cols):
            rows = x[b, g * K_PASS : (g + 1) * K_PASS, cols]
            nc.sync.dma_start(out=raw[(b, g)][:, :, cols], in_=rows.rearrange("(p j) t -> p j t", j=PACK))

        def load_weights():
            words = qkv_words.rearrange("m p n t -> m p (n t)").bitcast(I32)
            words = words.rearrange("(e g) p n -> g p e n", g=PASSES)
            scales = qkv_scales.bitcast(I32).rearrange("(e g) q n -> g q e n", g=PASSES)
            for g in range(PASSES):
                nc.sync.dma_start(
                    out=w_codes[:, g, :].bitcast(I32).rearrange("p (e n) -> p e n", e=MATRICES),
                    in_=words[g],
                )
            for g in range(PASSES):
                for quad in range(4):
                    nc.sync.dma_start(
                        out=w_planes[32 * quad : 32 * quad + 4, g, :]
                        .bitcast(I32)
                        .rearrange("r (e n) -> r e n", e=MATRICES),
                        in_=scales[g, 4 * quad : 4 * quad + 4],
                    )
            nc.sync.dma_start(out=gain_bf16[:], in_=norm_w.partition_broadcast(P))

        def chunk_cols(k):
            return slice(k * CHUNK, (k + 1) * CHUNK)

        make_room(0)
        for k in range(CHUNKS):
            for g in range(PASSES):
                load_x(0, g, chunk_cols(k))
        load_weights()
        for b in range(1, RAW_ROWS):
            make_room(b)
            for g in range(PASSES):
                load_x(b, g, slice(0, SEQ))

        nc.scalar.activation(out=partial_copy[:, 0:1], in_=eps[:], func=ACT.Abs_reciprocal_sqrt)
        nc.gpsimd.tensor_copy(out=gain[:], in_=gain_bf16[:])

        def leaky_relu(b, k, g):
            grouped = grouped_pool.tile([P, CHUNK, PACK], BF16, align_bytes=64)
            rows = raw[(b, g)][:, :, chunk_cols(k)].rearrange("p j t -> p t j")
            nc.vector.scalar_tensor_tensor(
                out=grouped[:], in0=rows, scalar=NEG_SLOPE, in1=rows, op0=ALU.mult, op1=ALU.max
            )
            return grouped

        def regroup_on_scalar(b, k, g):
            lifted = lifted_pool.tile([P, CHUNK, PACK], BF16, align_bytes=64)
            nc.scalar.copy(out=lifted[:], in_=raw[(b, g)][:, :, chunk_cols(k)].rearrange("p j t -> p t j"))
            return lifted

        def scale_down(lifted, holder):
            scaled = scaled_pool.tile([P, CHUNK * PACK], BF16)
            holder.append(scaled)
            nc.vector.tensor_scalar(
                out=scaled[:],
                in0=lifted[:].rearrange("p t j -> p (t j)"),
                scalar1=NEG_SLOPE,
                scalar2=None,
                op0=ALU.mult,
            )

        def take_larger(lifted, holder):
            flat = lifted[:].rearrange("p t j -> p (t j)")
            nc.vector.tensor_tensor(out=flat, in0=flat, in1=holder[0][:], op=ALU.max)

        quantised = {}
        passes_ready = {}

        def quantise(grouped, b, k, g):
            if (b, k) not in quantised:
                codes = code_pool.tile([P, PASSES, CHUNK], U32, tag="codes%d" % k, name="codes", align_bytes=64)
                planes = code_pool.tile([P, PASSES, CHUNK], U8, tag="planes%d" % k, name="planes", align_bytes=64)
                quantised[(b, k)] = (codes, planes)
            codes, planes = quantised[(b, k)]
            nc.vector.quantize_mx(
                out=codes[:, g, :].bitcast(FP8X4),
                scales=planes[:, g, :],
                in_=grouped[:].rearrange("p t j -> p (t j)"),
            )
            passes_ready[(b, k)] = passes_ready.get((b, k), 0) + 1

        pieces = [(b, k, g) for b in range(BATCH) for k in range(CHUNKS) for g in range(PASSES)]
        started = [0]
        unfinished = []

        def advance():
            for steps in unfinished:
                step, arguments = steps.pop(0)
                step(*arguments)
            for steps in [s for s in unfinished if not s]:
                unfinished.remove(steps)

        def start_next_piece():
            b, k, g = pieces[started[0]]
            started[0] += 1
            if b == 0 and g == (0 if k == CHUNKS - 1 else 1):
                advance()
                lifted = regroup_on_scalar(b, k, g)
                holder = []
                steps = [(scale_down, (lifted, holder)), (take_larger, (lifted, holder)), (quantise, (lifted, b, k, g))]
            else:
                steps = [(quantise, (leaky_relu(b, k, g), b, k, g))]
                advance()
            unfinished.append(steps)

        def ensure(b, k):
            while passes_ready.get((b, k), 0) < PASSES:
                if started[0] < len(pieces) and pieces[started[0]][0] == b:
                    start_next_piece()
                else:
                    advance()

        def take_bank(shape, name, index=None):
            return index, psum.tile(shape, F32, tag="bank", name=name)

        def multiply(units, b, k, index=None):
            codes, planes = quantised[(b, k)]
            banks = [take_bank([P, CHUNK], "product", index) for n in units]
            for g in range(PASSES):
                for n, (place, bank) in zip(units, banks):
                    w_cols = slice(n * UNIT_COLS, (n + 1) * UNIT_COLS)
                    nc.tensor.matmul_mx(
                        out=bank[:],
                        lhsT=w_codes[:, g, w_cols].bitcast(FP8X4),
                        lhsT_scale=w_planes[:, g, w_cols],
                        rhs=codes[:, g, :].bitcast(FP8X4),
                        rhs_scale=planes[:, g, :],
                        start=(g == 0),
                        stop=(g == PASSES - 1),
                    )
            return banks

        def add_squares(partial, b, k):
            ensure(b, k)
            banks = multiply(range(QKV), b, k)
            for n, (place, bank) in enumerate(banks):
                nc.scalar.activation(
                    out=squares[:], in_=bank[:], func=ACT.Square, accum_out=partial[:, n, k : k + 1]
                )
            return banks

        def reciprocal_rms(partial, on_vector):
            total = stat_pool.tile([P, QKV], F32)
            if on_vector:
                nc.vector.tensor_reduce(out=total[:], in_=partial[:], axis=mybir.AxisListType.X, op=ALU.add)
            else:
                for n in range(QKV):
                    nc.scalar.activation(
                        out=partial_copy[:], in_=partial[:, n, :], func=ACT.Copy, accum_out=total[:, n : n + 1]
                    )
            rrms = stat_pool.tile([P, QKV], F32)
            nc.scalar.activation(
                out=rrms[:], in_=total[:], func=ACT.Abs_reciprocal_sqrt, scale=1.0 / SEQ, bias=eps[:]
            )
            return rrms

        def empty_bank(on_vector, out_ap, in_ap, factor):
            if on_vector:
                nc.vector.tensor_scalar(out=out_ap, in0=in_ap, scalar1=factor, scalar2=None, op0=ALU.mult)
            else:
                nc.scalar.activation(out=out_ap, in_=in_ap, func=ACT.Copy, scale=factor)

        def normalise(n, bank, rrms, on_vector):
            normed = normed_pool.tile([P, TR_PER_BANK, P], F32)
            empty_bank(
                on_vector,
                normed[:],
                bank[:].rearrange("c (r s) -> c s r", s=TR_PER_BANK),
                rrms[:, n : n + 1],
            )
            return normed

        def flip(normed, index=None):
            place, bank = take_bank([P, TR_PER_BANK, P], "flipped", index)
            for s in range(TR_PER_BANK):
                nc.tensor.transpose(bank[:, s, :], normed[:, s, :], identity[:])
            return bank

        def store(b, n, k, bank, on_vector):
            result = result_pool.tile([P, HEADS, TR_PER_BANK, HEAD_DIM], F32)
            empty_bank(
                on_vector,
                result[:].rearrange("r i s j -> r s i j"),
                bank[:].rearrange("r s (i j) -> r s i j", i=HEADS),
                gain[:],
            )
            nc.sync.dma_start(
                out=out[n, b, :, chunk_cols(k), :].rearrange("i (r s) j -> r i (s j)", s=TR_PER_BANK),
                in_=result[:].rearrange("r i s j -> r i (s j)"),
            )

        def normalise_unit(b, n, rrms):
            return [normalise(n, multiply([n], b, k)[0][1], rrms, False) for k in range(CHUNKS)]

        def flip_and_store_unit(b, n, normed):
            for k in range(CHUNKS):
                store(b, n, k, flip(normed[k]), False)

        LAST = BATCH - 1
        partial = stat_pool.tile([P, QKV, CHUNKS], F32)
        ensure(0, CHUNKS - 1)
        for b in range(RAW_ROWS, BATCH):
            make_room(b)
            for g in range(PASSES):
                load_x(b, g, slice(0, SEQ))
        for k in range(CHUNKS):
            add_squares(partial, 0, k)
        rrms = reciprocal_rms(partial, False)
        waiting = None
        kept = []
        for b in range(LAST):
            partial = stat_pool.tile([P, QKV, CHUNKS], F32)
            for k in range(CHUNKS):
                if k < QKV:
                    normed = normalise_unit(b, k, rrms)
                    if waiting is not None:
                        flip_and_store_unit(*waiting)
                    waiting = (b, k, normed)
                keep = b + 1 == LAST and k >= CHUNKS - 2
                if keep and waiting is not None:
                    flip_and_store_unit(*waiting)
                    waiting = None
                if keep and k == CHUNKS - 1:
                    for n in range(PSUM_BANKS - 2 * QKV):
                        place, bank = multiply([n], LAST, 0)[0]
                        kept.append((0, n, place, bank))
                banks = add_squares(partial, b + 1, k)
                if keep:
                    for n, (place, bank) in enumerate(banks):
                        kept.append((k, n, place, bank))
            rrms = reciprocal_rms(partial, b + 1 == LAST)

        items = list(kept)
        missing = [(k, n) for k in range(CHUNKS) for n in range(QKV) if (k, n) not in [item[:2] for item in kept]]
        flipped = {}

        def normalise_and_flip(i):
            k, n, place, bank = items[i]
            flipped[i] = flip(normalise(n, bank, rrms, i % 2 == 1), place)

        def store_item(i):
            k, n, place, bank = items[i]
            store(LAST, n, k, flipped[i], i % 2 == 1)

        for i in range(len(kept)):
            normalise_and_flip(i)
        for i, (k, n) in enumerate(missing):
            store_item(i)
            place, bank = multiply([n], LAST, k, items[i][2])[0]
            items.append((k, n, place, bank))
        for i in range(len(missing)):
            normalise_and_flip(len(kept) + i)
            store_item(len(missing) + i)
        for i in range(len(kept), len(items)):
            store_item(i)
